import numpy as np
import ml_dtypes


def mxq(x, axis, fmt="e4m3"):
    dtype, down = {"e4m3": (ml_dtypes.float8_e4m3fn, 7), "e5m2": (ml_dtypes.float8_e5m2, 14)}[fmt]
    v = np.moveaxis(np.asarray(x, np.float32).astype(ml_dtypes.bfloat16).astype(np.float64), axis, -1)
    blocks = v.reshape(v.shape[:-1] + (-1, 32))
    amax = np.abs(blocks).max(-1, keepdims=True)
    byte = np.maximum(np.where(amax > 0, np.frexp(amax)[1] - 1 + 127, 0) - down, 1)
    scale = np.exp2(byte - 127.0)
    codes = (blocks / scale).astype(np.float32).astype(dtype).astype(np.float64)
    return np.moveaxis((codes * scale).reshape(v.shape), -1, axis)


WIDE = False


def mx_kscale(k):
    if not WIDE:
        return np.ones(k)
    levels = np.array([10, -10, 5, -5, 0])
    a = np.random.permutation(np.resize(levels, k // 512 * 4)).reshape(k // 512, 4)
    idx = np.arange(k)
    return np.exp2(a[idx // 512, idx % 128 // 32])


BF16 = ml_dtypes.bfloat16


def bf(x):
    return np.asarray(x, np.float32).astype(BF16)


def f64(x):
    return np.asarray(x).astype(np.float64)


B, IN, HID, N, NM = 64, 2, 62, 512, 5
C = IN + HID


def setup_inputs():
    s = mx_kscale(N)
    return {"x": bf(np.random.standard_normal((B, C, N)) * s),
            "support0": bf(np.random.standard_normal((N, N)) * 0.7 / np.sqrt(N) * s[:, None] / s[None, :]),
            "support1": bf(np.random.standard_normal((N, N)) * 0.7 / np.sqrt(N) * s[:, None] / s[None, :])}


def reference(x, support0, support1):
    x0 = f64(x)
    xq = mxq(x0, 2, "e4m3")
    a0q = mxq(f64(support0).T, 0, "e4m3")
    a1q = mxq(f64(support1).T, 0, "e4m3")
    x1_0 = xq @ a0q
    x2_0 = 2.0 * (mxq(x1_0, 2, "e4m3") @ a0q) - x0
    x1_1 = xq @ a1q
    x2_1 = 2.0 * (mxq(x1_1, 2, "e4m3") @ a1q) - x0
    return np.concatenate([x1_0, x2_0, x1_1, x2_1], axis=1)

@@ -1,0 +1,227 @@
+from contextlib import ExitStack
+
+import concourse.mybir as mybir
+from concourse.masks import make_identity
+
+F32 = mybir.dt.float32
+BF16 = mybir.dt.bfloat16
+U32 = mybir.dt.uint32
+U8 = mybir.dt.uint8
+FP8X4 = mybir.dt.float8_e4m3fn_x4
+MULT = mybir.AluOpType.mult
+SUBTRACT = mybir.AluOpType.subtract
+
+P = 128
+NODES = 512
+FLOPS = 4 * 2 * 4096 * 512 * 512
+
+MANUAL = False
+LAG = 2
+STAGE_BUFS = 12
+QUADS = 8
+STEPS = QUADS * 8
+V_E1 = ()
+
+
+def tile_dcgrucell_pa_t_kernel(tc, x, support0, support1, out):
+    nc = tc.nc
+    supports = (support0, support1)
+    x_v = x.flatten_outer_dims().rearrange(
+        "(s p h e) n -> s h p (e n)", s=4, p=P, h=2, e=4
+    )
+    out_v = out.rearrange(
+        "(s b) (q j h e) n -> s q h b j (e n)", b=16, q=4, j=8, h=2, e=4
+    )
+
+    with ExitStack() as ctx:
+        keep = ctx.enter_context(tc.tile_pool(name="keep", bufs=1))
+        grp = ctx.enter_context(tc.tile_pool(name="grp", bufs=3))
+        stp = ctx.enter_context(tc.tile_pool(name="stp", bufs=LAG + 2))
+        stage = ctx.enter_context(tc.tile_pool(name="stage", bufs=STAGE_BUFS))
+        psum = ctx.enter_context(tc.psum_pool(name="psum", bufs=2))
+        if MANUAL:
+            ctx.enter_context(tc.manual_schedule())
+
+        a_raw = []
+        xq = []
+        for a in range(2):
+            a_raw.append(keep.tile([P, 4 * NODES], BF16, name="a_raw%d" % a, tag="a_raw%d" % a))
+        for qd in range(QUADS):
+            xq.append(keep.tile([P, 4 * NODES], BF16, name="xq%d" % qd, tag="xq%d" % qd))
+
+        def load_a(a):
+            nc.sync.dma_start(
+                out=a_raw[a][:].rearrange("p (u f) -> p u f", u=2),
+                in_=supports[a].rearrange("(u p e) m -> p u (e m)", u=2, e=2),
+            )
+
+        def load_x(qd):
+            nc.sync.dma_start(out=xq[qd][:], in_=x_v[qd // 2, qd % 2])
+
+        load_a(0)
+        load_x(0)
+        load_a(1)
+        for qd in range(1, QUADS):
+            load_x(qd)
+
+        ident = keep.tile([P, P], F32, name="ident", tag="ident")
+        make_identity(nc, ident[:])
+
+        def vcopy(o, i):
+            nc.vector.tensor_copy(out=o, in_=i)
+
+        def scopy(o, i):
+            nc.scalar.copy(out=o, in_=i)
+
+        def transposes(src, pair):
+            words = src[:].bitcast(F32).rearrange("p (c w) -> p c w", c=4)
+            bank = psum.tile([P, 512], F32, name="tr", tag="tr")
+            for u in range(2):
+                for ee in range(2):
+                    col = (2 * u + ee) * P
+                    nc.tensor.transpose(
+                        bank[:, col : col + P],
+                        words[:, 2 * pair + ee, u * P : (u + 1) * P],
+                        ident[:],
+                    )
+            return bank
+
+        def evac_same_order(copy, bank, grouped, half):
+            copy(
+                grouped[:].bitcast(F32)[:, half * 512 : (half + 1) * 512].rearrange(
+                    "w (c u) -> w c u", u=2
+                ),
+                bank[:].rearrange("w (u c) -> w c u", u=2),
+            )
+
+        def evac_natural(copy, bank, grouped, half):
+            copy(
+                grouped[:].bitcast(F32)[:, half * 512 : (half + 1) * 512].rearrange(
+                    "w (p e u) -> w p e u", e=2, u=2
+                ),
+                bank[:].rearrange("w (u e p) -> w p e u", u=2, e=2),
+            )
+
+        def quantise(grouped, codes, scales):
+            nc.vector.quantize_mx(
+                out=codes.bitcast(FP8X4), scales=scales, in_=grouped
+            )
+
+        an_c, an_s, ap_c, ap_s = [], [], [], []
+        for a in range(2):
+            an_c.append(keep.tile([P, NODES], U32, name="an_c%d" % a, tag="an_c%d" % a, align_bytes=64))
+            an_s.append(keep.tile([P, NODES], U8, name="an_s%d" % a, tag="an_s%d" % a, align_bytes=64))
+            ap_c.append(keep.tile([P, NODES], U32, name="ap_c%d" % a, tag="ap_c%d" % a, align_bytes=64))
+            ap_s.append(keep.tile([P, NODES], U8, name="ap_s%d" % a, tag="ap_s%d" % a, align_bytes=64))
+        xc, xs = [], []
+        for qd in range(QUADS):
+            xc.append(keep.tile([P, 512], U32, name="xc%d" % qd, tag="xc%d" % qd, align_bytes=64))
+            xs.append(keep.tile([P, 512], U8, name="xs%d" % qd, tag="xs%d" % qd, align_bytes=64))
+
+        state = {}
+
+        def prep_a_pe(a):
+            state["abank"] = [transposes(a_raw[a], 0), transposes(a_raw[a], 1)]
+            state["gp"] = grp.tile([P, 2048], BF16, name="gp", tag="grp", align_bytes=64)
+            state["gn"] = grp.tile([P, 2048], BF16, name="gn", tag="grp", align_bytes=64)
+
+        def prep_a_evac(half, copy):
+            evac_same_order(copy, state["abank"][half], state["gp"], half)
+            evac_natural(copy, state["abank"][half], state["gn"], half)
+
+        def prep_a_quant(a):
+            quantise(state["gp"][:], ap_c[a][:], ap_s[a][:])
+            quantise(state["gn"][:], an_c[a][:], an_s[a][:])
+
+        def prep_x_pe(qd):
+            state["xbank"] = [transposes(xq[qd], 0), transposes(xq[qd], 1)]
+            state["gx"] = grp.tile([P, 2048], BF16, name="gx", tag="grp", align_bytes=64)
+
+        def prep_x_evac(half, copy):
+            evac_same_order(copy, state["xbank"][half], state["gx"], half)
+
+        def prep_x_quant(qd):
+            quantise(state["gx"][:], xc[qd][:], xs[qd][:])
+
+        prep_a_pe(0)
+        prep_a_evac(0, vcopy)
+        prep_a_evac(1, scopy)
+        prep_x_pe(0)
+        prep_a_quant(0)
+        prep_x_evac(0, scopy)
+        prep_x_evac(1, scopy)
+        prep_x_quant(0)
+
+        c1 = {}
+        s1 = {}
+        st1 = {}
+        st2 = {}
+
+        def mx(o, lc, ls, rc, rs):
+            nc.tensor.matmul_mx(
+                out=o,
+                lhsT=lc.bitcast(FP8X4),
+                lhsT_scale=ls,
+                rhs=rc.bitcast(FP8X4),
+                rhs_scale=rs,
+                start=True,
+                stop=True,
+            )
+
+        for j in range(STEPS + LAG):
+            if j < STEPS:
+                qd, a, e4 = j // 8, (j // 4) % 2, j % 4
+                cols = slice(e4 * P, (e4 + 1) * P)
+                t1 = psum.tile([P, 512], F32, name="t1", tag="t1")
+                for t in range(4):
+                    tc_ = slice(t * P, (t + 1) * P)
+                    mx(t1[:, tc_], ap_c[a][:, tc_], ap_s[a][:, tc_], xc[qd][:, cols], xs[qd][:, cols])
+                b1 = psum.tile([P, 512], F32, name="b1", tag="x1")
+                mx(b1[:], xc[qd][:, cols], xs[qd][:, cols], an_c[a][:], an_s[a][:])
+                g1 = stp.tile([P, 512], BF16, name="g1", tag="g1", align_bytes=64)
+                copy = vcopy if (j % 8) in V_E1 else scopy
+                copy(
+                    g1[:].rearrange("p (r t) -> p r t", t=4),
+                    t1[:].rearrange("p (t r) -> p r t", t=4),
+                )
+                if e4 == 0:
+                    st1[j // 4] = stage.tile([P, 4 * NODES], F32, name="st1", tag="st")
+                scopy(st1[j // 4][:, e4 * NODES : (e4 + 1) * NODES], b1[:])
+                c1[j] = stp.tile([P, P], U32, name="c1", tag="c1", align_bytes=64)
+                s1[j] = stp.tile([P, P], U8, name="s1", tag="s1", align_bytes=64)
+                quantise(g1[:], c1[j][:], s1[j][:])
+                if e4 == 3:
+                    nc.sync.dma_start(out=out_v[qd // 2, 2 * a, qd % 2], in_=st1[j // 4][:])
+            i = j - LAG
+            if i >= 0:
+                qd, a, e4 = i // 8, (i // 4) % 2, i % 4
+                b2 = psum.tile([P, 512], F32, name="b2", tag="x2")
+                mx(b2[:], c1[i][:], s1[i][:], an_c[a][:], an_s[a][:])
+                if e4 == 0:
+                    st2[i // 4] = stage.tile([P, 4 * NODES], F32, name="st2", tag="st")
+                nc.vector.scalar_tensor_tensor(
+                    out=st2[i // 4][:, e4 * NODES : (e4 + 1) * NODES],
+                    in0=b2[:],
+                    scalar=2.0,
+                    in1=xq[qd][:, e4 * NODES : (e4 + 1) * NODES],
+                    op0=MULT,
+                    op1=SUBTRACT,
+                )
+                if e4 == 3:
+                    nc.sync.dma_start(out=out_v[qd // 2, 2 * a + 1, qd % 2], in_=st2[i // 4][:])
+            if j == 0:
+                prep_a_pe(1)
+                prep_a_evac(0, vcopy)
+            if j == 1:
+                prep_a_evac(1, scopy)
+            if j == 2:
+                prep_a_quant(1)
+            nxt = j // 8 + 1
+            if nxt < QUADS:
+                if j % 8 == 3:
+                    prep_x_pe(nxt)
+                    prep_x_evac(0, vcopy)
+                if j % 8 == 4:
+                    prep_x_evac(1, vcopy)
+                if j % 8 == 5:
+                    prep_x_quant(nxt)

@@ -15,7 +15,7 @@ P = 128
 NODES = 512
 FLOPS = 4 * 2 * 4096 * 512 * 512
 
-MANUAL = False
+MANUAL = True
 LAG = 2
 STAGE_BUFS = 12
 QUADS = 8

@@ -20,7 +20,7 @@ LAG = 2
 STAGE_BUFS = 12
 QUADS = 8
 STEPS = QUADS * 8
-V_E1 = ()
+V_E1 = (1, 5)
 
 
 def tile_dcgrucell_pa_t_kernel(tc, x, support0, support1, out):
@@ -187,9 +187,6 @@ def tile_dcgrucell_pa_t_kernel(tc, x, support0, support1, out):
                 if e4 == 0:
                     st1[j // 4] = stage.tile([P, 4 * NODES], F32, name="st1", tag="st")
                 scopy(st1[j // 4][:, e4 * NODES : (e4 + 1) * NODES], b1[:])
-                c1[j] = stp.tile([P, P], U32, name="c1", tag="c1", align_bytes=64)
-                s1[j] = stp.tile([P, P], U8, name="s1", tag="s1", align_bytes=64)
-                quantise(g1[:], c1[j][:], s1[j][:])
                 if e4 == 3:
                     nc.sync.dma_start(out=out_v[qd // 2, 2 * a, qd % 2], in_=st1[j // 4][:])
             i = j - LAG
@@ -209,6 +206,10 @@ def tile_dcgrucell_pa_t_kernel(tc, x, support0, support1, out):
                 )
                 if e4 == 3:
                     nc.sync.dma_start(out=out_v[qd // 2, 2 * a + 1, qd % 2], in_=st2[i // 4][:])
+            if j < STEPS:
+                c1[j] = stp.tile([P, P], U32, name="c1", tag="c1", align_bytes=64)
+                s1[j] = stp.tile([P, P], U8, name="s1", tag="s1", align_bytes=64)
+                quantise(g1[:], c1[j][:], s1[j][:])
             if j == 0:
                 prep_a_pe(1)
                 prep_a_evac(0, vcopy)

@@ -39,6 +39,7 @@ def tile_dcgrucell_pa_t_kernel(tc, x, support0, support1, out):
         stp = ctx.enter_context(tc.tile_pool(name="stp", bufs=LAG + 2))
         stage = ctx.enter_context(tc.tile_pool(name="stage", bufs=STAGE_BUFS))
         psum = ctx.enter_context(tc.psum_pool(name="psum", bufs=2))
+        junkp = ctx.enter_context(tc.tile_pool(name="junkp", bufs=3))
         if MANUAL:
             ctx.enter_context(tc.manual_schedule())
 
@@ -178,6 +179,8 @@ def tile_dcgrucell_pa_t_kernel(tc, x, support0, support1, out):
                     mx(t1[:, tc_], ap_c[a][:, tc_], ap_s[a][:, tc_], xc[qd][:, cols], xs[qd][:, cols])
                 b1 = psum.tile([P, 512], F32, name="b1", tag="x1")
                 mx(b1[:], xc[qd][:, cols], xs[qd][:, cols], an_c[a][:], an_s[a][:])
+                if j % 2 == 0:
+                    mx(b1[:], xc[qd][:, cols], xs[qd][:, cols], an_c[a][:], an_s[a][:])
                 g1 = stp.tile([P, 512], BF16, name="g1", tag="g1", align_bytes=64)
                 copy = vcopy if (j % 8) in V_E1 else scopy
                 copy(
@@ -210,6 +213,9 @@ def tile_dcgrucell_pa_t_kernel(tc, x, support0, support1, out):
                 c1[j] = stp.tile([P, P], U32, name="c1", tag="c1", align_bytes=64)
                 s1[j] = stp.tile([P, P], U8, name="s1", tag="s1", align_bytes=64)
                 quantise(g1[:], c1[j][:], s1[j][:])
+            if j < STEPS and j % 8 in (1, 3, 5):
+                junk = junkp.tile([P, 4 * NODES], BF16, name="junk", tag="junk")
+                nc.sync.dma_start(out=junk[:], in_=x_v[(j // 8) // 2, (j // 8) % 2])
             if j == 0:
                 prep_a_pe(1)
                 prep_a_evac(0, vcopy)

@@ -27,10 +27,10 @@ def tile_dcgrucell_pa_t_kernel(tc, x, support0, support1, out):
     nc = tc.nc
     supports = (support0, support1)
     x_v = x.flatten_outer_dims().rearrange(
-        "(s p h e) n -> s h p (e n)", s=4, p=P, h=2, e=4
+        "(s p h e) n -> s h p (e n)", s=2, p=P, h=4, e=4
     )
     out_v = out.rearrange(
-        "(s b) (q j h e) n -> s q h b j (e n)", b=16, q=4, j=8, h=2, e=4
+        "(s b) (q j h e) n -> s q h b j (e n)", b=32, q=4, j=4, h=4, e=4
     )
 
     with ExitStack() as ctx:
@@ -39,7 +39,6 @@ def tile_dcgrucell_pa_t_kernel(tc, x, support0, support1, out):
         stp = ctx.enter_context(tc.tile_pool(name="stp", bufs=LAG + 2))
         stage = ctx.enter_context(tc.tile_pool(name="stage", bufs=STAGE_BUFS))
         psum = ctx.enter_context(tc.psum_pool(name="psum", bufs=2))
-        junkp = ctx.enter_context(tc.tile_pool(name="junkp", bufs=3))
         if MANUAL:
             ctx.enter_context(tc.manual_schedule())
 
@@ -57,7 +56,7 @@ def tile_dcgrucell_pa_t_kernel(tc, x, support0, support1, out):
             )
 
         def load_x(qd):
-            nc.sync.dma_start(out=xq[qd][:], in_=x_v[qd // 2, qd % 2])
+            nc.sync.dma_start(out=xq[qd][:], in_=x_v[qd // 4, qd % 4])
 
         load_a(0)
         load_x(0)
@@ -153,6 +152,11 @@ def tile_dcgrucell_pa_t_kernel(tc, x, support0, support1, out):
         prep_x_evac(1, scopy)
         prep_x_quant(0)
 
+        def store(dst, tile_):
+            nc.sync.dma_start(out=dst[8:24], in_=tile_[32:96, :])
+            nc.gpsimd.dma_start(out=dst[0:8], in_=tile_[0:32, :])
+            nc.gpsimd.dma_start(out=dst[24:32], in_=tile_[96:128, :])
+
         c1 = {}
         s1 = {}
         st1 = {}
@@ -191,7 +195,7 @@ def tile_dcgrucell_pa_t_kernel(tc, x, support0, support1, out):
                     st1[j // 4] = stage.tile([P, 4 * NODES], F32, name="st1", tag="st")
                 scopy(st1[j // 4][:, e4 * NODES : (e4 + 1) * NODES], b1[:])
                 if e4 == 3:
-                    nc.sync.dma_start(out=out_v[qd // 2, 2 * a, qd % 2], in_=st1[j // 4][:])
+                    store(out_v[qd // 4, 2 * a, qd % 4], st1[j // 4])
             i = j - LAG
             if i >= 0:
                 qd, a, e4 = i // 8, (i // 4) % 2, i % 4
@@ -208,14 +212,11 @@ def tile_dcgrucell_pa_t_kernel(tc, x, support0, support1, out):
                     op1=SUBTRACT,
                 )
                 if e4 == 3:
-                    nc.sync.dma_start(out=out_v[qd // 2, 2 * a + 1, qd % 2], in_=st2[i // 4][:])
+                    store(out_v[qd // 4, 2 * a + 1, qd % 4], st2[i // 4])
             if j < STEPS:
                 c1[j] = stp.tile([P, P], U32, name="c1", tag="c1", align_bytes=64)
                 s1[j] = stp.tile([P, P], U8, name="s1", tag="s1", align_bytes=64)
                 quantise(g1[:], c1[j][:], s1[j][:])
-            if j < STEPS and j % 8 in (1, 3, 5):
-                junk = junkp.tile([P, 4 * NODES], BF16, name="junk", tag="junk")
-                nc.sync.dma_start(out=junk[:], in_=x_v[(j // 8) // 2, (j // 8) % 2])
             if j == 0:
                 prep_a_pe(1)
                 prep_a_evac(0, vcopy)

@@ -15,23 +15,22 @@ P = 128
 NODES = 512
 FLOPS = 4 * 2 * 4096 * 512 * 512
 
-MANUAL = True
-LAG = 2
-STAGE_BUFS = 12
 QUADS = 8
-STEPS = QUADS * 8
-V_E1 = (1, 5)
+UNITS = 8
+STEPS = 8 * UNITS
+LAG = 2
+STAGE_BUFS = 7
+MID_TILES = 4
+VECTOR_E1 = 4
 
 
 def tile_dcgrucell_pa_t_kernel(tc, x, support0, support1, out):
     nc = tc.nc
     supports = (support0, support1)
     x_v = x.flatten_outer_dims().rearrange(
-        "(s p h e) n -> s h p (e n)", s=2, p=P, h=4, e=4
+        "(s p q e) n -> s q p (e n)", s=2, p=P, q=4, e=4
     )
-    out_v = out.rearrange(
-        "(s b) (q j h e) n -> s q h b j (e n)", b=32, q=4, j=4, h=4, e=4
-    )
+    out_v = out.rearrange("(s b) (k j e) n -> s k b j (e n)", b=32, k=4, j=4, e=16)
 
     with ExitStack() as ctx:
         keep = ctx.enter_context(tc.tile_pool(name="keep", bufs=1))
@@ -39,15 +38,14 @@ def tile_dcgrucell_pa_t_kernel(tc, x, support0, support1, out):
         stp = ctx.enter_context(tc.tile_pool(name="stp", bufs=LAG + 2))
         stage = ctx.enter_context(tc.tile_pool(name="stage", bufs=STAGE_BUFS))
         psum = ctx.enter_context(tc.psum_pool(name="psum", bufs=2))
-        if MANUAL:
-            ctx.enter_context(tc.manual_schedule())
+        ctx.enter_context(tc.manual_schedule())
 
         a_raw = []
         xq = []
         for a in range(2):
             a_raw.append(keep.tile([P, 4 * NODES], BF16, name="a_raw%d" % a, tag="a_raw%d" % a))
-        for qd in range(QUADS):
-            xq.append(keep.tile([P, 4 * NODES], BF16, name="xq%d" % qd, tag="xq%d" % qd))
+        for quad in range(QUADS):
+            xq.append(keep.tile([P, 4 * NODES], BF16, name="xq%d" % quad, tag="xq%d" % quad))
 
         def load_a(a):
             nc.sync.dma_start(
@@ -55,14 +53,15 @@ def tile_dcgrucell_pa_t_kernel(tc, x, support0, support1, out):
                 in_=supports[a].rearrange("(u p e) m -> p u (e m)", u=2, e=2),
             )
 
-        def load_x(qd):
-            nc.sync.dma_start(out=xq[qd][:], in_=x_v[qd // 4, qd % 4])
+        def load_x(quad):
+            nc.sync.dma_start(out=xq[quad][:], in_=x_v[quad // 4, quad % 4])
 
-        load_a(0)
         load_x(0)
+        load_a(0)
+        load_x(1)
         load_a(1)
-        for qd in range(1, QUADS):
-            load_x(qd)
+        for quad in range(2, QUADS):
+            load_x(quad)
 
         ident = keep.tile([P, P], F32, name="ident", tag="ident")
         make_identity(nc, ident[:])
@@ -73,9 +72,9 @@ def tile_dcgrucell_pa_t_kernel(tc, x, support0, support1, out):
         def scopy(o, i):
             nc.scalar.copy(out=o, in_=i)
 
-        def transposes(src, pair):
+        def transposes(src, pair, tag):
             words = src[:].bitcast(F32).rearrange("p (c w) -> p c w", c=4)
-            bank = psum.tile([P, 512], F32, name="tr", tag="tr")
+            bank = psum.tile([P, 512], F32, name="tr", tag=tag)
             for u in range(2):
                 for ee in range(2):
                     col = (2 * u + ee) * P
@@ -103,9 +102,7 @@ def tile_dcgrucell_pa_t_kernel(tc, x, support0, support1, out):
             )
 
         def quantise(grouped, codes, scales):
-            nc.vector.quantize_mx(
-                out=codes.bitcast(FP8X4), scales=scales, in_=grouped
-            )
+            nc.vector.quantize_mx(out=codes.bitcast(FP8X4), scales=scales, in_=grouped)
 
         an_c, an_s, ap_c, ap_s = [], [], [], []
         for a in range(2):
@@ -114,14 +111,14 @@ def tile_dcgrucell_pa_t_kernel(tc, x, support0, support1, out):
             ap_c.append(keep.tile([P, NODES], U32, name="ap_c%d" % a, tag="ap_c%d" % a, align_bytes=64))
             ap_s.append(keep.tile([P, NODES], U8, name="ap_s%d" % a, tag="ap_s%d" % a, align_bytes=64))
         xc, xs = [], []
-        for qd in range(QUADS):
-            xc.append(keep.tile([P, 512], U32, name="xc%d" % qd, tag="xc%d" % qd, align_bytes=64))
-            xs.append(keep.tile([P, 512], U8, name="xs%d" % qd, tag="xs%d" % qd, align_bytes=64))
+        for quad in range(QUADS):
+            xc.append(keep.tile([P, 512], U32, name="xc%d" % quad, tag="xc%d" % quad, align_bytes=64))
+            xs.append(keep.tile([P, 512], U8, name="xs%d" % quad, tag="xs%d" % quad, align_bytes=64))
 
         state = {}
 
-        def prep_a_pe(a):
-            state["abank"] = [transposes(a_raw[a], 0), transposes(a_raw[a], 1)]
+        def prep_a_pe(a, tag):
+            state["abank"] = [transposes(a_raw[a], 0, tag), transposes(a_raw[a], 1, tag)]
             state["gp"] = grp.tile([P, 2048], BF16, name="gp", tag="grp", align_bytes=64)
             state["gn"] = grp.tile([P, 2048], BF16, name="gn", tag="grp", align_bytes=64)
 
@@ -133,34 +130,28 @@ def tile_dcgrucell_pa_t_kernel(tc, x, support0, support1, out):
             quantise(state["gp"][:], ap_c[a][:], ap_s[a][:])
             quantise(state["gn"][:], an_c[a][:], an_s[a][:])
 
-        def prep_x_pe(qd):
-            state["xbank"] = [transposes(xq[qd], 0), transposes(xq[qd], 1)]
+        def prep_x_pe(quad):
+            state["xbank"] = [transposes(xq[quad], 0, "tr"), transposes(xq[quad], 1, "tr")]
             state["gx"] = grp.tile([P, 2048], BF16, name="gx", tag="grp", align_bytes=64)
 
         def prep_x_evac(half, copy):
             evac_same_order(copy, state["xbank"][half], state["gx"], half)
 
-        def prep_x_quant(qd):
-            quantise(state["gx"][:], xc[qd][:], xs[qd][:])
+        def prep_x_quant(quad):
+            quantise(state["gx"][:], xc[quad][:], xs[quad][:])
 
-        prep_a_pe(0)
-        prep_a_evac(0, vcopy)
-        prep_a_evac(1, scopy)
         prep_x_pe(0)
-        prep_a_quant(0)
-        prep_x_evac(0, scopy)
+        prep_a_pe(0, "x2")
+        prep_x_evac(0, vcopy)
         prep_x_evac(1, scopy)
         prep_x_quant(0)
+        prep_a_evac(0, vcopy)
+        prep_a_evac(1, scopy)
+        prep_a_quant(0)
 
-        def store(dst, tile_):
-            nc.sync.dma_start(out=dst[8:24], in_=tile_[32:96, :])
-            nc.gpsimd.dma_start(out=dst[0:8], in_=tile_[0:32, :])
-            nc.gpsimd.dma_start(out=dst[24:32], in_=tile_[96:128, :])
-
-        c1 = {}
-        s1 = {}
-        st1 = {}
-        st2 = {}
+        x_prep_step = {0: 1}
+        for quad in range(2, QUADS):
+            x_prep_step[8 * (quad - 2) + 6] = quad
 
         def mx(o, lc, ls, rc, rs):
             nc.tensor.matmul_mx(
@@ -173,63 +164,80 @@ def tile_dcgrucell_pa_t_kernel(tc, x, support0, support1, out):
                 stop=True,
             )
 
+        def where(step):
+            unit, e8 = step // 8, step % 8
+            e16 = 8 * ((unit // 2) % 2) + e8
+            return unit, e8, unit % 2, 4 * (unit // 4) + e16 // 4, e16 % 4
+
+        staged = {}
+
+        def staging(kind, unit, e8):
+            if e8 == 0:
+                staged[kind] = stage.tile([P, 8 * NODES], F32, name="st%d" % kind, tag="st")
+            return staged[kind][:, e8 * NODES : (e8 + 1) * NODES]
+
+        def store_if_full(kind, unit, e8):
+            dst = out_v[unit // 4, 2 * (unit % 2) + kind]
+            e0 = 8 * ((unit // 2) % 2)
+            if (e8 + 1) % MID_TILES == 0:
+                first = e8 + 1 - MID_TILES
+                here = slice(first * NODES, (e8 + 1) * NODES)
+                there = slice((e0 + first) * NODES, (e0 + e8 + 1) * NODES)
+                nc.sync.dma_start(out=dst[8:24, :, there], in_=staged[kind][32:96, here])
+            if e8 == 7:
+                there = slice(e0 * NODES, (e0 + 8) * NODES)
+                nc.gpsimd.dma_start(out=dst[0:8, :, there], in_=staged[kind][0:32, :])
+                nc.gpsimd.dma_start(out=dst[24:32, :, there], in_=staged[kind][96:128, :])
+
+        c1 = {}
+        s1 = {}
         for j in range(STEPS + LAG):
             if j < STEPS:
-                qd, a, e4 = j // 8, (j // 4) % 2, j % 4
+                unit, e8, a, quad, e4 = where(j)
                 cols = slice(e4 * P, (e4 + 1) * P)
                 t1 = psum.tile([P, 512], F32, name="t1", tag="t1")
                 for t in range(4):
-                    tc_ = slice(t * P, (t + 1) * P)
-                    mx(t1[:, tc_], ap_c[a][:, tc_], ap_s[a][:, tc_], xc[qd][:, cols], xs[qd][:, cols])
+                    chunk = slice(t * P, (t + 1) * P)
+                    mx(t1[:, chunk], ap_c[a][:, chunk], ap_s[a][:, chunk], xc[quad][:, cols], xs[quad][:, cols])
                 b1 = psum.tile([P, 512], F32, name="b1", tag="x1")
-                mx(b1[:], xc[qd][:, cols], xs[qd][:, cols], an_c[a][:], an_s[a][:])
-                if j % 2 == 0:
-                    mx(b1[:], xc[qd][:, cols], xs[qd][:, cols], an_c[a][:], an_s[a][:])
+                mx(b1[:], xc[quad][:, cols], xs[quad][:, cols], an_c[a][:], an_s[a][:])
                 g1 = stp.tile([P, 512], BF16, name="g1", tag="g1", align_bytes=64)
-                copy = vcopy if (j % 8) in V_E1 else scopy
+                copy = vcopy if j % 8 == VECTOR_E1 else scopy
                 copy(
                     g1[:].rearrange("p (r t) -> p r t", t=4),
                     t1[:].rearrange("p (t r) -> p r t", t=4),
                 )
-                if e4 == 0:
-                    st1[j // 4] = stage.tile([P, 4 * NODES], F32, name="st1", tag="st")
-                scopy(st1[j // 4][:, e4 * NODES : (e4 + 1) * NODES], b1[:])
-                if e4 == 3:
-                    store(out_v[qd // 4, 2 * a, qd % 4], st1[j // 4])
+                scopy(staging(0, unit, e8), b1[:])
+                store_if_full(0, unit, e8)
             i = j - LAG
             if i >= 0:
-                qd, a, e4 = i // 8, (i // 4) % 2, i % 4
+                unit, e8, a, quad, e4 = where(i)
                 b2 = psum.tile([P, 512], F32, name="b2", tag="x2")
                 mx(b2[:], c1[i][:], s1[i][:], an_c[a][:], an_s[a][:])
-                if e4 == 0:
-                    st2[i // 4] = stage.tile([P, 4 * NODES], F32, name="st2", tag="st")
                 nc.vector.scalar_tensor_tensor(
-                    out=st2[i // 4][:, e4 * NODES : (e4 + 1) * NODES],
+                    out=staging(1, unit, e8),
                     in0=b2[:],
                     scalar=2.0,
-                    in1=xq[qd][:, e4 * NODES : (e4 + 1) * NODES],
+                    in1=xq[quad][:, e4 * NODES : (e4 + 1) * NODES],
                     op0=MULT,
                     op1=SUBTRACT,
                 )
-                if e4 == 3:
-                    store(out_v[qd // 4, 2 * a + 1, qd % 4], st2[i // 4])
+                store_if_full(1, unit, e8)
             if j < STEPS:
                 c1[j] = stp.tile([P, P], U32, name="c1", tag="c1", align_bytes=64)
                 s1[j] = stp.tile([P, P], U8, name="s1", tag="s1", align_bytes=64)
                 quantise(g1[:], c1[j][:], s1[j][:])
-            if j == 0:
-                prep_a_pe(1)
+            if j in x_prep_step:
+                prep_x_pe(x_prep_step[j])
+                prep_x_evac(0, vcopy)
+            if j - 1 in x_prep_step:
+                prep_x_evac(1, vcopy)
+            if j - 2 in x_prep_step:
+                prep_x_quant(x_prep_step[j - 2])
+            if j == 3:
+                prep_a_pe(1, "tr")
                 prep_a_evac(0, vcopy)
-            if j == 1:
+            if j == 4:
                 prep_a_evac(1, scopy)
-            if j == 2:
+            if j == 5:
                 prep_a_quant(1)
-            nxt = j // 8 + 1
-            if nxt < QUADS:
-                if j % 8 == 3:
-                    prep_x_pe(nxt)
-                    prep_x_evac(0, vcopy)
-                if j % 8 == 4:
-                    prep_x_evac(1, vcopy)
-                if j % 8 == 5:
-                    prep_x_quant(nxt)

@@ -18,7 +18,7 @@ FLOPS = 4 * 2 * 4096 * 512 * 512
 QUADS = 8
 UNITS = 8
 STEPS = 8 * UNITS
-LAG = 2
+LAG = 3
 STAGE_BUFS = 7
 MID_TILES = 4
 VECTOR_E1 = 4
@@ -34,7 +34,7 @@ def tile_dcgrucell_pa_t_kernel(tc, x, support0, support1, out):
 
     with ExitStack() as ctx:
         keep = ctx.enter_context(tc.tile_pool(name="keep", bufs=1))
-        grp = ctx.enter_context(tc.tile_pool(name="grp", bufs=3))
+        grp = ctx.enter_context(tc.tile_pool(name="grp", bufs=4))
         stp = ctx.enter_context(tc.tile_pool(name="stp", bufs=LAG + 2))
         stage = ctx.enter_context(tc.tile_pool(name="stage", bufs=STAGE_BUFS))
         psum = ctx.enter_context(tc.psum_pool(name="psum", bufs=2))
@@ -115,41 +115,44 @@ def tile_dcgrucell_pa_t_kernel(tc, x, support0, support1, out):
             xc.append(keep.tile([P, 512], U32, name="xc%d" % quad, tag="xc%d" % quad, align_bytes=64))
             xs.append(keep.tile([P, 512], U8, name="xs%d" % quad, tag="xs%d" % quad, align_bytes=64))
 
-        state = {}
+        abank, gp, gn, xbank, gx = {}, {}, {}, {}, {}
 
         def prep_a_pe(a, tag):
-            state["abank"] = [transposes(a_raw[a], 0, tag), transposes(a_raw[a], 1, tag)]
-            state["gp"] = grp.tile([P, 2048], BF16, name="gp", tag="grp", align_bytes=64)
-            state["gn"] = grp.tile([P, 2048], BF16, name="gn", tag="grp", align_bytes=64)
+            abank[a] = [transposes(a_raw[a], 0, tag), transposes(a_raw[a], 1, tag)]
+            gp[a] = grp.tile([P, 2048], BF16, name="gp", tag="grp", align_bytes=64)
+            gn[a] = grp.tile([P, 2048], BF16, name="gn", tag="grp", align_bytes=64)
 
-        def prep_a_evac(half, copy):
-            evac_same_order(copy, state["abank"][half], state["gp"], half)
-            evac_natural(copy, state["abank"][half], state["gn"], half)
+        def prep_a_evac(a, half, copy):
+            evac_same_order(copy, abank[a][half], gp[a], half)
+            evac_natural(copy, abank[a][half], gn[a], half)
 
         def prep_a_quant(a):
-            quantise(state["gp"][:], ap_c[a][:], ap_s[a][:])
-            quantise(state["gn"][:], an_c[a][:], an_s[a][:])
+            quantise(gp[a][:], ap_c[a][:], ap_s[a][:])
+            quantise(gn[a][:], an_c[a][:], an_s[a][:])
 
-        def prep_x_pe(quad):
-            state["xbank"] = [transposes(xq[quad], 0, "tr"), transposes(xq[quad], 1, "tr")]
-            state["gx"] = grp.tile([P, 2048], BF16, name="gx", tag="grp", align_bytes=64)
+        def prep_x_pe(quad, tag):
+            xbank[quad] = [transposes(xq[quad], 0, tag), transposes(xq[quad], 1, tag)]
+            gx[quad] = grp.tile([P, 2048], BF16, name="gx", tag="grp", align_bytes=64)
 
-        def prep_x_evac(half, copy):
-            evac_same_order(copy, state["xbank"][half], state["gx"], half)
+        def prep_x_evac(quad, half, copy):
+            evac_same_order(copy, xbank[quad][half], gx[quad], half)
 
         def prep_x_quant(quad):
-            quantise(state["gx"][:], xc[quad][:], xs[quad][:])
+            quantise(gx[quad][:], xc[quad][:], xs[quad][:])
 
-        prep_x_pe(0)
+        prep_x_pe(0, "tr")
         prep_a_pe(0, "x2")
-        prep_x_evac(0, vcopy)
-        prep_x_evac(1, scopy)
+        prep_x_pe(1, "x1")
+        prep_x_evac(0, 0, vcopy)
+        prep_x_evac(0, 1, scopy)
         prep_x_quant(0)
-        prep_a_evac(0, vcopy)
-        prep_a_evac(1, scopy)
+        prep_a_evac(0, 0, vcopy)
+        prep_a_evac(0, 1, scopy)
         prep_a_quant(0)
+        prep_x_evac(1, 0, scopy)
+        prep_x_evac(1, 1, scopy)
 
-        x_prep_step = {0: 1}
+        x_prep_step = {}
         for quad in range(2, QUADS):
             x_prep_step[8 * (quad - 2) + 6] = quad
 
@@ -227,17 +230,19 @@ def tile_dcgrucell_pa_t_kernel(tc, x, support0, support1, out):
                 c1[j] = stp.tile([P, P], U32, name="c1", tag="c1", align_bytes=64)
                 s1[j] = stp.tile([P, P], U8, name="s1", tag="s1", align_bytes=64)
                 quantise(g1[:], c1[j][:], s1[j][:])
+            if j == 0:
+                prep_x_quant(1)
             if j in x_prep_step:
-                prep_x_pe(x_prep_step[j])
-                prep_x_evac(0, vcopy)
+                prep_x_pe(x_prep_step[j], "tr")
+                prep_x_evac(x_prep_step[j], 0, vcopy)
             if j - 1 in x_prep_step:
-                prep_x_evac(1, vcopy)
+                prep_x_evac(x_prep_step[j - 1], 1, vcopy)
             if j - 2 in x_prep_step:
                 prep_x_quant(x_prep_step[j - 2])
-            if j == 3:
+            if j == 2:
                 prep_a_pe(1, "tr")
-                prep_a_evac(0, vcopy)
-            if j == 4:
-                prep_a_evac(1, scopy)
+                prep_a_evac(1, 0, vcopy)
+            if j == 3:
+                prep_a_evac(1, 1, scopy)
             if j == 5:
                 prep_a_quant(1)

@@ -18,7 +18,7 @@ FLOPS = 4 * 2 * 4096 * 512 * 512
 QUADS = 8
 UNITS = 8
 STEPS = 8 * UNITS
-LAG = 3
+LAG = 2
 STAGE_BUFS = 7
 MID_TILES = 4
 VECTOR_E1 = 4
@@ -187,10 +187,13 @@ def tile_dcgrucell_pa_t_kernel(tc, x, support0, support1, out):
                 here = slice(first * NODES, (e8 + 1) * NODES)
                 there = slice((e0 + first) * NODES, (e0 + e8 + 1) * NODES)
                 nc.sync.dma_start(out=dst[8:24, :, there], in_=staged[kind][32:96, here])
-            if e8 == 7:
-                there = slice(e0 * NODES, (e0 + 8) * NODES)
-                nc.gpsimd.dma_start(out=dst[0:8, :, there], in_=staged[kind][0:32, :])
-                nc.gpsimd.dma_start(out=dst[24:32, :, there], in_=staged[kind][96:128, :])
+            side_tiles = 4 if unit < 2 else 8
+            if (e8 + 1) % side_tiles == 0:
+                first = e8 + 1 - side_tiles
+                here = slice(first * NODES, (e8 + 1) * NODES)
+                there = slice((e0 + first) * NODES, (e0 + e8 + 1) * NODES)
+                nc.gpsimd.dma_start(out=dst[0:8, :, there], in_=staged[kind][0:32, here])
+                nc.gpsimd.dma_start(out=dst[24:32, :, there], in_=staged[kind][96:128, here])
 
         c1 = {}
         s1 = {}

from contextlib import ExitStack

import concourse.mybir as mybir
from concourse.masks import make_identity

F32 = mybir.dt.float32
BF16 = mybir.dt.bfloat16
U32 = mybir.dt.uint32
U8 = mybir.dt.uint8
FP8X4 = mybir.dt.float8_e4m3fn_x4
MULT = mybir.AluOpType.mult
SUBTRACT = mybir.AluOpType.subtract

P = 128
NODES = 512
FLOPS = 4 * 2 * 4096 * 512 * 512

QUADS = 8
UNITS = 8
STEPS = 8 * UNITS
LAG = 2
STAGE_BUFS = 7
MID_TILES = 4
VECTOR_E1 = 4


def tile_dcgrucell_pa_t_kernel(tc, x, support0, support1, out):
    nc = tc.nc
    supports = (support0, support1)
    x_v = x.flatten_outer_dims().rearrange(
        "(s p q e) n -> s q p (e n)", s=2, p=P, q=4, e=4
    )
    out_v = out.rearrange("(s b) (k j e) n -> s k b j (e n)", b=32, k=4, j=4, e=16)

    with ExitStack() as ctx:
        keep = ctx.enter_context(tc.tile_pool(name="keep", bufs=1))
        grp = ctx.enter_context(tc.tile_pool(name="grp", bufs=4))
        stp = ctx.enter_context(tc.tile_pool(name="stp", bufs=LAG + 2))
        stage = ctx.enter_context(tc.tile_pool(name="stage", bufs=STAGE_BUFS))
        psum = ctx.enter_context(tc.psum_pool(name="psum", bufs=2))
        ctx.enter_context(tc.manual_schedule())

        a_raw = []
        xq = []
        for a in range(2):
            a_raw.append(keep.tile([P, 4 * NODES], BF16, name="a_raw%d" % a, tag="a_raw%d" % a))
        for quad in range(QUADS):
            xq.append(keep.tile([P, 4 * NODES], BF16, name="xq%d" % quad, tag="xq%d" % quad))

        def load_a(a):
            nc.sync.dma_start(
                out=a_raw[a][:].rearrange("p (u f) -> p u f", u=2),
                in_=supports[a].rearrange("(u p e) m -> p u (e m)", u=2, e=2),
            )

        def load_x(quad):
            nc.sync.dma_start(out=xq[quad][:], in_=x_v[quad // 4, quad % 4])

        load_x(0)
        load_a(0)
        load_x(1)
        load_a(1)
        for quad in range(2, QUADS):
            load_x(quad)

        ident = keep.tile([P, P], F32, name="ident", tag="ident")
        make_identity(nc, ident[:])

        def vcopy(o, i):
            nc.vector.tensor_copy(out=o, in_=i)

        def scopy(o, i):
            nc.scalar.copy(out=o, in_=i)

        def transposes(src, pair, tag):
            words = src[:].bitcast(F32).rearrange("p (c w) -> p c w", c=4)
            bank = psum.tile([P, 512], F32, name="tr", tag=tag)
            for u in range(2):
                for ee in range(2):
                    col = (2 * u + ee) * P
                    nc.tensor.transpose(
                        bank[:, col : col + P],
                        words[:, 2 * pair + ee, u * P : (u + 1) * P],
                        ident[:],
                    )
            return bank

        def evac_same_order(copy, bank, grouped, half):
            copy(
                grouped[:].bitcast(F32)[:, half * 512 : (half + 1) * 512].rearrange(
                    "w (c u) -> w c u", u=2
                ),
                bank[:].rearrange("w (u c) -> w c u", u=2),
            )

        def evac_natural(copy, bank, grouped, half):
            copy(
                grouped[:].bitcast(F32)[:, half * 512 : (half + 1) * 512].rearrange(
                    "w (p e u) -> w p e u", e=2, u=2
                ),
                bank[:].rearrange("w (u e p) -> w p e u", u=2, e=2),
            )

        def quantise(grouped, codes, scales):
            nc.vector.quantize_mx(out=codes.bitcast(FP8X4), scales=scales, in_=grouped)

        an_c, an_s, ap_c, ap_s = [], [], [], []
        for a in range(2):
            an_c.append(keep.tile([P, NODES], U32, name="an_c%d" % a, tag="an_c%d" % a, align_bytes=64))
            an_s.append(keep.tile([P, NODES], U8, name="an_s%d" % a, tag="an_s%d" % a, align_bytes=64))
            ap_c.append(keep.tile([P, NODES], U32, name="ap_c%d" % a, tag="ap_c%d" % a, align_bytes=64))
            ap_s.append(keep.tile([P, NODES], U8, name="ap_s%d" % a, tag="ap_s%d" % a, align_bytes=64))
        xc, xs = [], []
        for quad in range(QUADS):
            xc.append(keep.tile([P, 512], U32, name="xc%d" % quad, tag="xc%d" % quad, align_bytes=64))
            xs.append(keep.tile([P, 512], U8, name="xs%d" % quad, tag="xs%d" % quad, align_bytes=64))

        abank, gp, gn, xbank, gx = {}, {}, {}, {}, {}

        def prep_a_pe(a, tag):
            abank[a] = [transposes(a_raw[a], 0, tag), transposes(a_raw[a], 1, tag)]
            gp[a] = grp.tile([P, 2048], BF16, name="gp", tag="grp", align_bytes=64)
            gn[a] = grp.tile([P, 2048], BF16, name="gn", tag="grp", align_bytes=64)

        def prep_a_evac(a, half, copy):
            evac_same_order(copy, abank[a][half], gp[a], half)
            evac_natural(copy, abank[a][half], gn[a], half)

        def prep_a_quant(a):
            quantise(gp[a][:], ap_c[a][:], ap_s[a][:])
            quantise(gn[a][:], an_c[a][:], an_s[a][:])

        def prep_x_pe(quad, tag):
            xbank[quad] = [transposes(xq[quad], 0, tag), transposes(xq[quad], 1, tag)]
            gx[quad] = grp.tile([P, 2048], BF16, name="gx", tag="grp", align_bytes=64)

        def prep_x_evac(quad, half, copy):
            evac_same_order(copy, xbank[quad][half], gx[quad], half)

        def prep_x_quant(quad):
            quantise(gx[quad][:], xc[quad][:], xs[quad][:])

        prep_x_pe(0, "tr")
        prep_a_pe(0, "x2")
        prep_x_pe(1, "x1")
        prep_x_evac(0, 0, vcopy)
        prep_x_evac(0, 1, scopy)
        prep_x_quant(0)
        prep_a_evac(0, 0, vcopy)
        prep_a_evac(0, 1, scopy)
        prep_a_quant(0)
        prep_x_evac(1, 0, scopy)
        prep_x_evac(1, 1, scopy)

        x_prep_step = {}
        for quad in range(2, QUADS):
            x_prep_step[8 * (quad - 2) + 6] = quad

        def mx(o, lc, ls, rc, rs):
            nc.tensor.matmul_mx(
                out=o,
                lhsT=lc.bitcast(FP8X4),
                lhsT_scale=ls,
                rhs=rc.bitcast(FP8X4),
                rhs_scale=rs,
                start=True,
                stop=True,
            )

        def where(step):
            unit, e8 = step // 8, step % 8
            e16 = 8 * ((unit // 2) % 2) + e8
            return unit, e8, unit % 2, 4 * (unit // 4) + e16 // 4, e16 % 4

        staged = {}

        def staging(kind, unit, e8):
            if e8 == 0:
                staged[kind] = stage.tile([P, 8 * NODES], F32, name="st%d" % kind, tag="st")
            return staged[kind][:, e8 * NODES : (e8 + 1) * NODES]

        def store_if_full(kind, unit, e8):
            dst = out_v[unit // 4, 2 * (unit % 2) + kind]
            e0 = 8 * ((unit // 2) % 2)
            if (e8 + 1) % MID_TILES == 0:
                first = e8 + 1 - MID_TILES
                here = slice(first * NODES, (e8 + 1) * NODES)
                there = slice((e0 + first) * NODES, (e0 + e8 + 1) * NODES)
                nc.sync.dma_start(out=dst[8:24, :, there], in_=staged[kind][32:96, here])
            side_tiles = 4 if unit < 2 else 8
            if (e8 + 1) % side_tiles == 0:
                first = e8 + 1 - side_tiles
                here = slice(first * NODES, (e8 + 1) * NODES)
                there = slice((e0 + first) * NODES, (e0 + e8 + 1) * NODES)
                nc.gpsimd.dma_start(out=dst[0:8, :, there], in_=staged[kind][0:32, here])
                nc.gpsimd.dma_start(out=dst[24:32, :, there], in_=staged[kind][96:128, here])

        c1 = {}
        s1 = {}
        for j in range(STEPS + LAG):
            if j < STEPS:
                unit, e8, a, quad, e4 = where(j)
                cols = slice(e4 * P, (e4 + 1) * P)
                t1 = psum.tile([P, 512], F32, name="t1", tag="t1")
                for t in range(4):
                    chunk = slice(t * P, (t + 1) * P)
                    mx(t1[:, chunk], ap_c[a][:, chunk], ap_s[a][:, chunk], xc[quad][:, cols], xs[quad][:, cols])
                b1 = psum.tile([P, 512], F32, name="b1", tag="x1")
                mx(b1[:], xc[quad][:, cols], xs[quad][:, cols], an_c[a][:], an_s[a][:])
                g1 = stp.tile([P, 512], BF16, name="g1", tag="g1", align_bytes=64)
                copy = vcopy if j % 8 == VECTOR_E1 else scopy
                copy(
                    g1[:].rearrange("p (r t) -> p r t", t=4),
                    t1[:].rearrange("p (t r) -> p r t", t=4),
                )
                scopy(staging(0, unit, e8), b1[:])
                store_if_full(0, unit, e8)
            i = j - LAG
            if i >= 0:
                unit, e8, a, quad, e4 = where(i)
                b2 = psum.tile([P, 512], F32, name="b2", tag="x2")
                mx(b2[:], c1[i][:], s1[i][:], an_c[a][:], an_s[a][:])
                nc.vector.scalar_tensor_tensor(
                    out=staging(1, unit, e8),
                    in0=b2[:],
                    scalar=2.0,
                    in1=xq[quad][:, e4 * NODES : (e4 + 1) * NODES],
                    op0=MULT,
                    op1=SUBTRACT,
                )
                store_if_full(1, unit, e8)
            if j < STEPS:
                c1[j] = stp.tile([P, P], U32, name="c1", tag="c1", align_bytes=64)
                s1[j] = stp.tile([P, P], U8, name="s1", tag="s1", align_bytes=64)
                quantise(g1[:], c1[j][:], s1[j][:])
            if j == 0:
                prep_x_quant(1)
            if j in x_prep_step:
                prep_x_pe(x_prep_step[j], "tr")
                prep_x_evac(x_prep_step[j], 0, vcopy)
            if j - 1 in x_prep_step:
                prep_x_evac(x_prep_step[j - 1], 1, vcopy)
            if j - 2 in x_prep_step:
                prep_x_quant(x_prep_step[j - 2])
            if j == 2:
                prep_a_pe(1, "tr")
                prep_a_evac(1, 0, vcopy)
            if j == 3:
                prep_a_evac(1, 1, scopy)
            if j == 5:
                prep_a_quant(1)
